import numpy as np
import ml_dtypes


def mxq(x, axis, fmt="e4m3"):
    dtype, down = {"e4m3": (ml_dtypes.float8_e4m3fn, 7), "e5m2": (ml_dtypes.float8_e5m2, 14)}[fmt]
    v = np.moveaxis(np.asarray(x, np.float32).astype(ml_dtypes.bfloat16).astype(np.float64), axis, -1)
    blocks = v.reshape(v.shape[:-1] + (-1, 32))
    amax = np.abs(blocks).max(-1, keepdims=True)
    byte = np.maximum(np.where(amax > 0, np.frexp(amax)[1] - 1 + 127, 0) - down, 1)
    scale = np.exp2(byte - 127.0)
    codes = (blocks / scale).astype(np.float32).astype(dtype).astype(np.float64)
    return np.moveaxis((codes * scale).reshape(v.shape), -1, axis)


WIDE = False


def mx_kscale(k):
    if not WIDE:
        return np.ones(k)
    levels = np.array([10, -10, 5, -5, 0])
    a = np.random.permutation(np.resize(levels, k // 512 * 4)).reshape(k // 512, 4)
    idx = np.arange(k)
    return np.exp2(a[idx // 512, idx % 128 // 32])


BF16 = ml_dtypes.bfloat16


def bf(x):
    return np.asarray(x, np.float32).astype(BF16)


def f64(x):
    return np.asarray(x).astype(np.float64)


E2M1 = np.array([0.0, 0.5, 1.0, 1.5, 2.0, 3.0, 4.0, 6.0, -0.0, -0.5, -1.0, -1.5, -2.0, -3.0, -4.0, -6.0])


def pack_weight(w, fmt):
    k, n = w.shape
    w = f64(bf(w)).reshape(k // 32, 32, n)
    amax = np.abs(w).max(1)
    if fmt == "e4m3":
        byte = np.frexp(amax)[1] - 1 + 127 - 7
    else:
        mant, ex = np.frexp(amax / 6.0)
        byte = np.where(mant > 0.5, ex, ex - 1) + 127
    byte = np.clip(np.where(amax > 0, byte, 1), 1, 254)
    scaled = (w * np.exp2(127.0 - byte)[:, None, :]).reshape(k, n).astype(np.float32)
    by_word = np.ascontiguousarray(scaled.reshape(k // 512, 128, 4, n).transpose(0, 1, 3, 2))
    if fmt == "e4m3":
        words = by_word.astype(ml_dtypes.float8_e4m3fn).view(np.uint8)
    else:
        c = by_word.astype(ml_dtypes.float4_e2m1fn).view(np.uint8) & 0xF
        words = c[..., 0::2] | (c[..., 1::2] << 4)
    return np.ascontiguousarray(words), np.ascontiguousarray(byte.astype(np.uint8).reshape(k // 512, 16, n))


def unpack_weight(words, scales, fmt):
    g, p, n, _ = words.shape
    if fmt == "e4m3":
        vals = np.ascontiguousarray(words).view(ml_dtypes.float8_e4m3fn).astype(np.float64)
    else:
        nib = np.empty((g, p, n, 4), np.uint8)
        nib[..., 0::2] = words & 0xF
        nib[..., 1::2] = words >> 4
        vals = E2M1[nib]
    vals = vals * np.repeat(np.exp2(scales.astype(np.float64) - 127.0), 8, axis=1)[..., None]
    return vals.transpose(0, 1, 3, 2).reshape(g * 512, n)

def pack4(w):
    words, scales = pack_weight(w, "e2m1")
    return words.reshape(words.shape[0], 128, -1), scales


def unpack4(words, scales):
    return unpack_weight(words.reshape(words.shape[0], 128, -1, 2), scales, "e2m1")


B, T, D, H, KV, DH = 2, 64, 8192, 16, 4, 128
G = H // KV
HALF = DH // 2
ROPE_THETA = 1e6
YARN_FACTOR = 64.0
ORIG_MAX_POS = 4096.0
BETA_FAST, BETA_SLOW = 4.0, 1.0
ATTN_FACTOR = 0.1 * np.log(YARN_FACTOR) + 1.0


def corr_dim(num_rot):
    return DH * np.log(ORIG_MAX_POS / (num_rot * 2 * np.pi)) / (2 * np.log(ROPE_THETA))


def yarn_inv_freq():
    low = float(np.sum(np.arange(DH) + 1 <= corr_dim(BETA_FAST)))
    high = min(float(np.sum(np.arange(DH) < corr_dim(BETA_SLOW))), DH - 1.0)
    if low == high:
        high += 0.001
    ramp = np.clip((np.arange(HALF) - low) / (high - low), 0.0, 1.0)
    pos_freqs = ROPE_THETA ** (np.arange(0, DH, 2) / DH)
    inv_extrap = 1.0 / pos_freqs
    inv_interp = 1.0 / (YARN_FACTOR * pos_freqs)
    extrap_factor = 1.0 - ramp
    return inv_interp * (1.0 - extrap_factor) + inv_extrap * extrap_factor


def rope_yarn(v):
    angles = np.arange(T)[:, None] * yarn_inv_freq()[None, :]
    cos = np.cos(angles)[None, :, None, :]
    sin = np.sin(angles)[None, :, None, :]
    v_even = v[..., 0::2]
    v_odd = v[..., 1::2]
    out_even = v_even * cos - v_odd * sin
    out_odd = v_even * sin + v_odd * cos
    return np.stack([out_even, out_odd], axis=-1).reshape(v.shape) * ATTN_FACTOR


def setup_inputs():
    s = mx_kscale(D)
    x = bf(np.random.standard_normal((B, T, D)) * s)
    words, scales = pack4(np.random.standard_normal((D, (H + 2 * KV) * DH)) / np.sqrt(D) / s[:, None])
    return {"x": x, "w_qkv_words": words, "w_qkv_scales": scales}


def reference(x, w_qkv_words, w_qkv_scales):
    qkv = mxq(f64(x), 2, "e4m3") @ unpack4(w_qkv_words, w_qkv_scales)
    q = qkv[:, :, :H * DH].reshape(B, T, H, DH)
    k = qkv[:, :, H * DH:(H + KV) * DH].reshape(B, T, KV, DH)
    v = qkv[:, :, (H + KV) * DH:].reshape(B, T, KV, DH)
    q = rope_yarn(q)
    k = rope_yarn(k)
    q = q.reshape(B, T, KV, G, DH).transpose(0, 2, 3, 1, 4)
    k = k.transpose(0, 2, 1, 3)
    v = v.transpose(0, 2, 1, 3)
    return q, k, v

@@ -1,0 +1,235 @@
+import math
+from contextlib import ExitStack
+
+import concourse.mybir as mybir
+from concourse.masks import make_identity
+
+F32 = mybir.dt.float32
+BF16 = mybir.dt.bfloat16
+I32 = mybir.dt.int32
+U32 = mybir.dt.uint32
+U8 = mybir.dt.uint8
+FP8X4 = mybir.dt.float8_e4m3fn_x4
+FP4X4 = mybir.dt.float4_e2m1fn_x4
+ALU = mybir.AluOpType
+ACT = mybir.ActivationFunctionType
+
+P = 128
+BATCH = 2
+POSITIONS = 64
+K = 8192
+K_PASS = 512
+PASSES = K // K_PASS
+HEAD = 128
+HALF = HEAD // 2
+DOUBLINGS = 6
+BANK = 512
+BANK_HEADS = BANK // HEAD
+Q_BANKS = 4
+KV_BANKS = 2
+COLS = (Q_BANKS + KV_BANKS) * BANK
+WORD_BYTES = 2
+
+X_LOADS = 4
+X_LOAD_PASSES = PASSES // X_LOADS
+PAIR = 2
+PLANE_PASSES = 4
+SCALE_ROWS = 16
+
+ROPE_THETA = 1e6
+YARN_FACTOR = 64.0
+RAMP_LOW = 23.0
+RAMP_WIDTH = 8.0
+ATTN_FACTOR = 0.1 * math.log(YARN_FACTOR) + 1.0
+TWO_PI = 2.0 * math.pi
+ROUND_MAGIC = 1.5 * 2.0**23
+ROTATION = ((1.0, math.pi / 2), (-1.0, 0.0), (1.0, 0.0), (1.0, math.pi / 2))
+
+FLOPS = 2 * P * K * COLS
+
+
+def build_rotation_table(nc, pool):
+    column_int = pool.tile([P, HALF], I32)
+    nc.gpsimd.iota(column_int[:], pattern=[[1, HALF]], base=0, channel_multiplier=0)
+    token_int = pool.tile([P, 1], I32)
+    nc.gpsimd.iota(token_int[:], pattern=[[1, 1]], base=0, channel_multiplier=1)
+
+    position_int = pool.tile([P, 1], I32)
+    nc.vector.tensor_single_scalar(position_int[:], token_int[:], POSITIONS - 1, op=ALU.bitwise_and)
+    position = pool.tile([P, 1], F32)
+    nc.vector.tensor_copy(out=position[:], in_=position_int[:])
+    column = pool.tile([P, HALF], F32)
+    nc.vector.tensor_copy(out=column[:], in_=column_int[:])
+
+    blend = pool.tile([P, HALF], F32)
+    nc.vector.tensor_scalar(
+        blend[:], column[:], 1.0 / RAMP_WIDTH, -RAMP_LOW / RAMP_WIDTH, op0=ALU.mult, op1=ALU.add
+    )
+    nc.vector.tensor_scalar(blend[:], blend[:], 0.0, 1.0, op0=ALU.max, op1=ALU.min)
+    nc.vector.tensor_scalar(
+        blend[:], blend[:], 1.0 / YARN_FACTOR - 1.0, 1.0, op0=ALU.mult, op1=ALU.add
+    )
+
+    frequency = pool.tile([P, HALF], F32)
+    nc.vector.memset(frequency[:, 0:1], 1.0)
+    for doubling in range(DOUBLINGS):
+        width = 2**doubling
+        nc.vector.tensor_scalar_mul(
+            frequency[:, width : 2 * width], frequency[:, 0:width], ROPE_THETA ** (-width / HALF)
+        )
+    nc.vector.tensor_mul(frequency[:], frequency[:], blend[:])
+
+    angle = pool.tile([P, HALF], F32)
+    nc.vector.tensor_scalar_mul(angle[:], frequency[:], position[:, 0:1])
+    argument = pool.tile([P, len(ROTATION), HALF], F32)
+    for j, (sign, phase) in enumerate(ROTATION):
+        nc.vector.tensor_scalar(argument[:, j, :], angle[:], sign, phase, op0=ALU.mult, op1=ALU.add)
+
+    turns = pool.tile([P, len(ROTATION), HALF], F32)
+    nc.vector.tensor_scalar(
+        turns[:], argument[:], 1.0 / TWO_PI, ROUND_MAGIC, op0=ALU.mult, op1=ALU.add
+    )
+    nc.vector.tensor_scalar(turns[:], turns[:], ROUND_MAGIC, -TWO_PI, op0=ALU.subtract, op1=ALU.mult)
+    nc.vector.tensor_add(argument[:], argument[:], turns[:])
+
+    table = pool.tile([P, 2, 2, HALF], F32)
+    flat_table = table[:].rearrange("p e s i -> p (e s) i")
+    nc.scalar.activation(out=flat_table, in_=argument[:], func=ACT.Sin)
+    nc.scalar.mul(flat_table, flat_table, ATTN_FACTOR)
+    return table
+
+
+def rotate_heads(nc, pool, bank, table, heads):
+    values = bank[:].rearrange("p (h i s) -> p s h i", h=BANK_HEADS, s=2)
+    products = pool.tile([P, 2, 2, BANK_HEADS, HALF], F32)
+    for e in range(2):
+        factors = table[:, e].unsqueeze(2).to_broadcast([P, 2, BANK_HEADS, HALF])
+        nc.vector.tensor_mul(products[:, e], values, factors)
+    nc.vector.tensor_add(
+        heads[:].rearrange("p h (i e) -> p h i e", e=2),
+        products[:, :, 0].rearrange("p e h i -> p h i e"),
+        products[:, :, 1].rearrange("p e h i -> p h i e"),
+    )
+
+
+def store_heads(queue, heads, dest):
+    for b in range(BATCH):
+        queue.dma_start(
+            out=dest[b].rearrange("h t d -> t h d"),
+            in_=heads[b * POSITIONS : (b + 1) * POSITIONS],
+        )
+
+
+def tile_causalselfattentiongqa_pa_k_kernel(
+    tc, x, w_qkv_words, w_qkv_scales, out_0, out_1, out_2
+):
+    nc = tc.nc
+    with ExitStack() as ctx:
+        ctx.enter_context(tc.manual_schedule())
+        keep = ctx.enter_context(tc.tile_pool(name="keep", bufs=1))
+        stage = ctx.enter_context(tc.tile_pool(name="stage", bufs=4))
+        results = ctx.enter_context(tc.tile_pool(name="results", bufs=Q_BANKS + KV_BANKS))
+        psum = ctx.enter_context(tc.psum_pool(name="psum", bufs=8))
+
+        identity = keep.tile([P, P], F32)
+        make_identity(nc, identity[:])
+
+        x_flat = x.rearrange("b t k -> (b t) k")
+        x_cols = K // X_LOADS
+        x_parts = []
+        for c in range(X_LOADS):
+            x_part = keep.tile([P, x_cols], BF16, name="x_part%d" % c)
+            nc.sync.dma_start(out=x_part[:], in_=x_flat[:, c * x_cols : (c + 1) * x_cols])
+            x_parts.append(x_part)
+
+        scale_rows = w_qkv_scales.bitcast(I32).rearrange("g (h q) n -> q h g n", h=2)
+        w_planes = []
+        for c in range(PASSES // PLANE_PASSES):
+            planes = keep.tile([P, PLANE_PASSES, COLS], U8, name="w_planes%d" % c, align_bytes=64)
+            nc.vector.memset(planes[:].bitcast(I32), 0)
+            w_planes.append(planes)
+        for c, planes in enumerate(w_planes):
+            for q in range(SCALE_ROWS // 2):
+                first = 32 * (q // 4) + q % 4
+                nc.sync.dma_start(
+                    out=planes[:].bitcast(I32)[first:P:64],
+                    in_=scale_rows[q, :, c * PLANE_PASSES : (c + 1) * PLANE_PASSES, :],
+                )
+
+        words = w_qkv_words.bitcast(I32)
+        q_ints = Q_BANKS * BANK * WORD_BYTES // 4
+        kv_ints = KV_BANKS * BANK * WORD_BYTES // 4
+        q_words = []
+        for g in range(PASSES):
+            part = keep.tile([P, Q_BANKS * BANK * WORD_BYTES], U8, name="q_words%d" % g, align_bytes=64)
+            nc.sync.dma_start(out=part[:].bitcast(I32), in_=words[g, :, 0:q_ints])
+            q_words.append(part)
+        kv_words = []
+        for g in range(PASSES):
+            part = keep.tile([P, KV_BANKS * BANK * WORD_BYTES], U8, name="kv_words%d" % g, align_bytes=64)
+            nc.sync.dma_start(out=part[:].bitcast(I32), in_=words[g, :, q_ints : q_ints + kv_ints])
+            kv_words.append(part)
+
+        x_codes = keep.tile([P, PASSES, P], U32, align_bytes=64)
+        x_scales = keep.tile([P, PASSES, P], U8, align_bytes=64)
+        for j in range(PASSES // PAIR):
+            turned = psum.tile([P, PAIR, 2, P], F32, tag="bank")
+            for s in range(PAIR):
+                g = j * PAIR + s
+                x_words = x_parts[g // X_LOAD_PASSES][:].bitcast(F32)
+                start = (g % X_LOAD_PASSES) * (K_PASS // 2)
+                for u in range(2):
+                    nc.tensor.transpose(
+                        turned[:, s, u, :],
+                        x_words[:, start + u : start + K_PASS // 2 : 2],
+                        identity[:],
+                    )
+            grouped = stage.tile([P, PAIR * P * 4], BF16, align_bytes=64)
+            nc.scalar.copy(
+                out=grouped[:].bitcast(F32).rearrange("p (s r u) -> p s r u", s=PAIR, u=2),
+                in_=turned[:].rearrange("p s u r -> p s r u"),
+            )
+            pair = slice(j * PAIR, (j + 1) * PAIR)
+            nc.vector.quantize_mx(
+                out=x_codes[:, pair, :].rearrange("p s r -> p (s r)").bitcast(FP8X4),
+                scales=x_scales[:, pair, :].rearrange("p s r -> p (s r)"),
+                in_=grouped[:],
+            )
+
+        table = build_rotation_table(nc, keep)
+
+        def multiply(g, bank, part, part_bank, first_col):
+            nc.tensor.matmul_mx(
+                out=bank[:],
+                lhsT=x_codes[:, g, :].bitcast(FP8X4),
+                lhsT_scale=x_scales[:, g, :],
+                rhs=part[
+                    :, part_bank * BANK * WORD_BYTES : (part_bank + 1) * BANK * WORD_BYTES
+                ].bitcast(FP4X4),
+                rhs_scale=w_planes[g // PLANE_PASSES][
+                    :, g % PLANE_PASSES, first_col : first_col + BANK
+                ],
+                start=(g == 0),
+                stop=(g == PASSES - 1),
+            )
+
+        q_banks = [psum.tile([P, BANK], F32, tag="bank", name="q_bank%d" % n) for n in range(Q_BANKS)]
+        for g in range(PASSES):
+            for n in range(Q_BANKS):
+                multiply(g, q_banks[n], q_words[g], n, n * BANK)
+        for n in range(Q_BANKS):
+            heads = results.tile([P, BANK_HEADS, HEAD], F32, tag="heads")
+            rotate_heads(nc, stage, q_banks[n], table, heads)
+            store_heads(nc.scalar, heads, out_0[:, n])
+
+        k_bank = psum.tile([P, BANK], F32, tag="bank")
+        v_bank = psum.tile([P, BANK], F32, tag="bank")
+        for g in range(PASSES):
+            multiply(g, k_bank, kv_words[g], 0, Q_BANKS * BANK)
+            multiply(g, v_bank, kv_words[g], 1, (Q_BANKS + 1) * BANK)
+        v_heads = results.tile([P, BANK_HEADS, HEAD], F32, tag="heads")
+        nc.scalar.copy(out=v_heads[:].rearrange("p h d -> p (h d)"), in_=v_bank[:])
+        store_heads(nc.scalar, v_heads, out_2)
+        k_heads = results.tile([P, BANK_HEADS, HEAD], F32, tag="heads")
+        rotate_heads(nc, stage, k_bank, table, k_heads)
+        store_heads(nc.sync, k_heads, out_1)

@@ -220,7 +220,7 @@ def tile_causalselfattentiongqa_pa_k_kernel(
         for n in range(Q_BANKS):
             heads = results.tile([P, BANK_HEADS, HEAD], F32, tag="heads")
             rotate_heads(nc, stage, q_banks[n], table, heads)
-            store_heads(nc.scalar, heads, out_0[:, n])
+            store_heads(nc.sync, heads, out_0[:, n])
 
         k_bank = psum.tile([P, BANK], F32, tag="bank")
         v_bank = psum.tile([P, BANK], F32, tag="bank")

@@ -55,7 +55,7 @@ def build_rotation_table(nc, pool):
     nc.gpsimd.iota(token_int[:], pattern=[[1, 1]], base=0, channel_multiplier=1)
 
     position_int = pool.tile([P, 1], I32)
-    nc.vector.tensor_single_scalar(position_int[:], token_int[:], POSITIONS - 1, op=ALU.bitwise_and)
+    nc.vector.tensor_single_scalar(position_int[:], token_int[:], 1, op=ALU.logical_shift_right)
     position = pool.tile([P, 1], F32)
     nc.vector.tensor_copy(out=position[:], in_=position_int[:])
     column = pool.tile([P, HALF], F32)
@@ -116,7 +116,7 @@ def store_heads(queue, heads, dest):
     for b in range(BATCH):
         queue.dma_start(
             out=dest[b].rearrange("h t d -> t h d"),
-            in_=heads[b * POSITIONS : (b + 1) * POSITIONS],
+            in_=heads[b:P:BATCH],
         )
 
 
@@ -134,12 +134,12 @@ def tile_causalselfattentiongqa_pa_k_kernel(
         identity = keep.tile([P, P], F32)
         make_identity(nc, identity[:])
 
-        x_flat = x.rearrange("b t k -> (b t) k")
+        x_tokens = x.rearrange("b t k -> t b k")
         x_cols = K // X_LOADS
         x_parts = []
         for c in range(X_LOADS):
             x_part = keep.tile([P, x_cols], BF16, name="x_part%d" % c)
-            nc.sync.dma_start(out=x_part[:], in_=x_flat[:, c * x_cols : (c + 1) * x_cols])
+            nc.sync.dma_start(out=x_part[:], in_=x_tokens[:, :, c * x_cols : (c + 1) * x_cols])
             x_parts.append(x_part)
 
         scale_rows = w_qkv_scales.bitcast(I32).rearrange("g (h q) n -> q h g n", h=2)

@@ -34,6 +34,7 @@ X_LOADS = 4
 X_LOAD_PASSES = PASSES // X_LOADS
 PAIR = 2
 PLANE_PASSES = 4
+EARLY_KEY_PASSES = 4
 SCALE_ROWS = 16
 
 ROPE_THETA = 1e6
@@ -159,15 +160,21 @@ def tile_causalselfattentiongqa_pa_k_kernel(
         words = w_qkv_words.bitcast(I32)
         q_ints = Q_BANKS * BANK * WORD_BYTES // 4
         kv_ints = KV_BANKS * BANK * WORD_BYTES // 4
+        bank_ints = BANK * WORD_BYTES // 4
+        first_early = PASSES - EARLY_KEY_PASSES
         q_words = []
         for g in range(PASSES):
-            part = keep.tile([P, Q_BANKS * BANK * WORD_BYTES], U8, name="q_words%d" % g, align_bytes=64)
-            nc.sync.dma_start(out=part[:].bitcast(I32), in_=words[g, :, 0:q_ints])
+            ints = q_ints + (bank_ints if g >= first_early else 0)
+            part = keep.tile([P, 4 * ints], U8, name="q_words%d" % g, align_bytes=64)
+            nc.sync.dma_start(out=part[:].bitcast(I32), in_=words[g, :, 0:ints])
             q_words.append(part)
         kv_words = []
         for g in range(PASSES):
-            part = keep.tile([P, KV_BANKS * BANK * WORD_BYTES], U8, name="kv_words%d" % g, align_bytes=64)
-            nc.sync.dma_start(out=part[:].bitcast(I32), in_=words[g, :, q_ints : q_ints + kv_ints])
+            skipped = bank_ints if g >= first_early else 0
+            part = keep.tile([P, 4 * (kv_ints - skipped)], U8, name="kv_words%d" % g, align_bytes=64)
+            nc.sync.dma_start(
+                out=part[:].bitcast(I32), in_=words[g, :, q_ints + skipped : q_ints + kv_ints]
+            )
             kv_words.append(part)
 
         x_codes = keep.tile([P, PASSES, P], U32, align_bytes=64)
@@ -198,7 +205,7 @@ def tile_causalselfattentiongqa_pa_k_kernel(
 
         table = build_rotation_table(nc, keep)
 
-        def multiply(g, bank, part, part_bank, first_col):
+        def multiply(g, bank, part, part_bank, first_col, start, stop):
             nc.tensor.matmul_mx(
                 out=bank[:],
                 lhsT=x_codes[:, g, :].bitcast(FP8X4),
@@ -209,27 +216,33 @@ def tile_causalselfattentiongqa_pa_k_kernel(
                 rhs_scale=w_planes[g // PLANE_PASSES][
                     :, g % PLANE_PASSES, first_col : first_col + BANK
                 ],
-                start=(g == 0),
-                stop=(g == PASSES - 1),
+                start=start,
+                stop=stop,
             )
 
         q_banks = [psum.tile([P, BANK], F32, tag="bank", name="q_bank%d" % n) for n in range(Q_BANKS)]
+        k_bank = psum.tile([P, BANK], F32, tag="bank")
         for g in range(PASSES):
             for n in range(Q_BANKS):
-                multiply(g, q_banks[n], q_words[g], n, n * BANK)
+                multiply(g, q_banks[n], q_words[g], n, n * BANK, g == 0, g == PASSES - 1)
+            if g >= first_early:
+                multiply(g, k_bank, q_words[g], Q_BANKS, Q_BANKS * BANK, g == first_early, False)
         for n in range(Q_BANKS):
             heads = results.tile([P, BANK_HEADS, HEAD], F32, tag="heads")
             rotate_heads(nc, stage, q_banks[n], table, heads)
             store_heads(nc.sync, heads, out_0[:, n])
 
-        k_bank = psum.tile([P, BANK], F32, tag="bank")
         v_bank = psum.tile([P, BANK], F32, tag="bank")
         for g in range(PASSES):
-            multiply(g, k_bank, kv_words[g], 0, Q_BANKS * BANK)
-            multiply(g, v_bank, kv_words[g], 1, (Q_BANKS + 1) * BANK)
-        v_heads = results.tile([P, BANK_HEADS, HEAD], F32, tag="heads")
-        nc.scalar.copy(out=v_heads[:].rearrange("p h d -> p (h d)"), in_=v_bank[:])
-        store_heads(nc.scalar, v_heads, out_2)
+            if g < first_early:
+                multiply(g, k_bank, kv_words[g], 0, Q_BANKS * BANK, False, g == first_early - 1)
+            multiply(
+                g, v_bank, kv_words[g], 1 if g < first_early else 0, (Q_BANKS + 1) * BANK,
+                g == 0, g == PASSES - 1,
+            )
         k_heads = results.tile([P, BANK_HEADS, HEAD], F32, tag="heads")
         rotate_heads(nc, stage, k_bank, table, k_heads)
         store_heads(nc.sync, k_heads, out_1)
+        v_heads = results.tile([P, BANK_HEADS, HEAD], F32, tag="heads")
+        nc.scalar.copy(out=v_heads[:].rearrange("p h d -> p (h d)"), in_=v_bank[:])
+        store_heads(nc.scalar, v_heads, out_2)

import math
from contextlib import ExitStack

import concourse.mybir as mybir
from concourse.masks import make_identity

F32 = mybir.dt.float32
BF16 = mybir.dt.bfloat16
I32 = mybir.dt.int32
U32 = mybir.dt.uint32
U8 = mybir.dt.uint8
FP8X4 = mybir.dt.float8_e4m3fn_x4
FP4X4 = mybir.dt.float4_e2m1fn_x4
ALU = mybir.AluOpType
ACT = mybir.ActivationFunctionType

P = 128
BATCH = 2
POSITIONS = 64
K = 8192
K_PASS = 512
PASSES = K // K_PASS
HEAD = 128
HALF = HEAD // 2
DOUBLINGS = 6
BANK = 512
BANK_HEADS = BANK // HEAD
Q_BANKS = 4
KV_BANKS = 2
COLS = (Q_BANKS + KV_BANKS) * BANK
WORD_BYTES = 2

X_LOADS = 4
X_LOAD_PASSES = PASSES // X_LOADS
PAIR = 2
PLANE_PASSES = 4
EARLY_KEY_PASSES = 4
SCALE_ROWS = 16

ROPE_THETA = 1e6
YARN_FACTOR = 64.0
RAMP_LOW = 23.0
RAMP_WIDTH = 8.0
ATTN_FACTOR = 0.1 * math.log(YARN_FACTOR) + 1.0
TWO_PI = 2.0 * math.pi
ROUND_MAGIC = 1.5 * 2.0**23
ROTATION = ((1.0, math.pi / 2), (-1.0, 0.0), (1.0, 0.0), (1.0, math.pi / 2))

FLOPS = 2 * P * K * COLS


def build_rotation_table(nc, pool):
    column_int = pool.tile([P, HALF], I32)
    nc.gpsimd.iota(column_int[:], pattern=[[1, HALF]], base=0, channel_multiplier=0)
    token_int = pool.tile([P, 1], I32)
    nc.gpsimd.iota(token_int[:], pattern=[[1, 1]], base=0, channel_multiplier=1)

    position_int = pool.tile([P, 1], I32)
    nc.vector.tensor_single_scalar(position_int[:], token_int[:], 1, op=ALU.logical_shift_right)
    position = pool.tile([P, 1], F32)
    nc.vector.tensor_copy(out=position[:], in_=position_int[:])
    column = pool.tile([P, HALF], F32)
    nc.vector.tensor_copy(out=column[:], in_=column_int[:])

    blend = pool.tile([P, HALF], F32)
    nc.vector.tensor_scalar(
        blend[:], column[:], 1.0 / RAMP_WIDTH, -RAMP_LOW / RAMP_WIDTH, op0=ALU.mult, op1=ALU.add
    )
    nc.vector.tensor_scalar(blend[:], blend[:], 0.0, 1.0, op0=ALU.max, op1=ALU.min)
    nc.vector.tensor_scalar(
        blend[:], blend[:], 1.0 / YARN_FACTOR - 1.0, 1.0, op0=ALU.mult, op1=ALU.add
    )

    frequency = pool.tile([P, HALF], F32)
    nc.vector.memset(frequency[:, 0:1], 1.0)
    for doubling in range(DOUBLINGS):
        width = 2**doubling
        nc.vector.tensor_scalar_mul(
            frequency[:, width : 2 * width], frequency[:, 0:width], ROPE_THETA ** (-width / HALF)
        )
    nc.vector.tensor_mul(frequency[:], frequency[:], blend[:])

    angle = pool.tile([P, HALF], F32)
    nc.vector.tensor_scalar_mul(angle[:], frequency[:], position[:, 0:1])
    argument = pool.tile([P, len(ROTATION), HALF], F32)
    for j, (sign, phase) in enumerate(ROTATION):
        nc.vector.tensor_scalar(argument[:, j, :], angle[:], sign, phase, op0=ALU.mult, op1=ALU.add)

    turns = pool.tile([P, len(ROTATION), HALF], F32)
    nc.vector.tensor_scalar(
        turns[:], argument[:], 1.0 / TWO_PI, ROUND_MAGIC, op0=ALU.mult, op1=ALU.add
    )
    nc.vector.tensor_scalar(turns[:], turns[:], ROUND_MAGIC, -TWO_PI, op0=ALU.subtract, op1=ALU.mult)
    nc.vector.tensor_add(argument[:], argument[:], turns[:])

    table = pool.tile([P, 2, 2, HALF], F32)
    flat_table = table[:].rearrange("p e s i -> p (e s) i")
    nc.scalar.activation(out=flat_table, in_=argument[:], func=ACT.Sin)
    nc.scalar.mul(flat_table, flat_table, ATTN_FACTOR)
    return table


def rotate_heads(nc, pool, bank, table, heads):
    values = bank[:].rearrange("p (h i s) -> p s h i", h=BANK_HEADS, s=2)
    products = pool.tile([P, 2, 2, BANK_HEADS, HALF], F32)
    for e in range(2):
        factors = table[:, e].unsqueeze(2).to_broadcast([P, 2, BANK_HEADS, HALF])
        nc.vector.tensor_mul(products[:, e], values, factors)
    nc.vector.tensor_add(
        heads[:].rearrange("p h (i e) -> p h i e", e=2),
        products[:, :, 0].rearrange("p e h i -> p h i e"),
        products[:, :, 1].rearrange("p e h i -> p h i e"),
    )


def store_heads(queue, heads, dest):
    for b in range(BATCH):
        queue.dma_start(
            out=dest[b].rearrange("h t d -> t h d"),
            in_=heads[b:P:BATCH],
        )


def tile_causalselfattentiongqa_pa_k_kernel(
    tc, x, w_qkv_words, w_qkv_scales, out_0, out_1, out_2
):
    nc = tc.nc
    with ExitStack() as ctx:
        ctx.enter_context(tc.manual_schedule())
        keep = ctx.enter_context(tc.tile_pool(name="keep", bufs=1))
        stage = ctx.enter_context(tc.tile_pool(name="stage", bufs=4))
        results = ctx.enter_context(tc.tile_pool(name="results", bufs=Q_BANKS + KV_BANKS))
        psum = ctx.enter_context(tc.psum_pool(name="psum", bufs=8))

        identity = keep.tile([P, P], F32)
        make_identity(nc, identity[:])

        x_tokens = x.rearrange("b t k -> t b k")
        x_cols = K // X_LOADS
        x_parts = []
        for c in range(X_LOADS):
            x_part = keep.tile([P, x_cols], BF16, name="x_part%d" % c)
            nc.sync.dma_start(out=x_part[:], in_=x_tokens[:, :, c * x_cols : (c + 1) * x_cols])
            x_parts.append(x_part)

        scale_rows = w_qkv_scales.bitcast(I32).rearrange("g (h q) n -> q h g n", h=2)
        w_planes = []
        for c in range(PASSES // PLANE_PASSES):
            planes = keep.tile([P, PLANE_PASSES, COLS], U8, name="w_planes%d" % c, align_bytes=64)
            nc.vector.memset(planes[:].bitcast(I32), 0)
            w_planes.append(planes)
        for c, planes in enumerate(w_planes):
            for q in range(SCALE_ROWS // 2):
                first = 32 * (q // 4) + q % 4
                nc.sync.dma_start(
                    out=planes[:].bitcast(I32)[first:P:64],
                    in_=scale_rows[q, :, c * PLANE_PASSES : (c + 1) * PLANE_PASSES, :],
                )

        words = w_qkv_words.bitcast(I32)
        q_ints = Q_BANKS * BANK * WORD_BYTES // 4
        kv_ints = KV_BANKS * BANK * WORD_BYTES // 4
        bank_ints = BANK * WORD_BYTES // 4
        first_early = PASSES - EARLY_KEY_PASSES
        q_words = []
        for g in range(PASSES):
            ints = q_ints + (bank_ints if g >= first_early else 0)
            part = keep.tile([P, 4 * ints], U8, name="q_words%d" % g, align_bytes=64)
            nc.sync.dma_start(out=part[:].bitcast(I32), in_=words[g, :, 0:ints])
            q_words.append(part)
        kv_words = []
        for g in range(PASSES):
            skipped = bank_ints if g >= first_early else 0
            part = keep.tile([P, 4 * (kv_ints - skipped)], U8, name="kv_words%d" % g, align_bytes=64)
            nc.sync.dma_start(
                out=part[:].bitcast(I32), in_=words[g, :, q_ints + skipped : q_ints + kv_ints]
            )
            kv_words.append(part)

        x_codes = keep.tile([P, PASSES, P], U32, align_bytes=64)
        x_scales = keep.tile([P, PASSES, P], U8, align_bytes=64)
        for j in range(PASSES // PAIR):
            turned = psum.tile([P, PAIR, 2, P], F32, tag="bank")
            for s in range(PAIR):
                g = j * PAIR + s
                x_words = x_parts[g // X_LOAD_PASSES][:].bitcast(F32)
                start = (g % X_LOAD_PASSES) * (K_PASS // 2)
                for u in range(2):
                    nc.tensor.transpose(
                        turned[:, s, u, :],
                        x_words[:, start + u : start + K_PASS // 2 : 2],
                        identity[:],
                    )
            grouped = stage.tile([P, PAIR * P * 4], BF16, align_bytes=64)
            nc.scalar.copy(
                out=grouped[:].bitcast(F32).rearrange("p (s r u) -> p s r u", s=PAIR, u=2),
                in_=turned[:].rearrange("p s u r -> p s r u"),
            )
            pair = slice(j * PAIR, (j + 1) * PAIR)
            nc.vector.quantize_mx(
                out=x_codes[:, pair, :].rearrange("p s r -> p (s r)").bitcast(FP8X4),
                scales=x_scales[:, pair, :].rearrange("p s r -> p (s r)"),
                in_=grouped[:],
            )

        table = build_rotation_table(nc, keep)

        def multiply(g, bank, part, part_bank, first_col, start, stop):
            nc.tensor.matmul_mx(
                out=bank[:],
                lhsT=x_codes[:, g, :].bitcast(FP8X4),
                lhsT_scale=x_scales[:, g, :],
                rhs=part[
                    :, part_bank * BANK * WORD_BYTES : (part_bank + 1) * BANK * WORD_BYTES
                ].bitcast(FP4X4),
                rhs_scale=w_planes[g // PLANE_PASSES][
                    :, g % PLANE_PASSES, first_col : first_col + BANK
                ],
                start=start,
                stop=stop,
            )

        q_banks = [psum.tile([P, BANK], F32, tag="bank", name="q_bank%d" % n) for n in range(Q_BANKS)]
        k_bank = psum.tile([P, BANK], F32, tag="bank")
        for g in range(PASSES):
            for n in range(Q_BANKS):
                multiply(g, q_banks[n], q_words[g], n, n * BANK, g == 0, g == PASSES - 1)
            if g >= first_early:
                multiply(g, k_bank, q_words[g], Q_BANKS, Q_BANKS * BANK, g == first_early, False)
        for n in range(Q_BANKS):
            heads = results.tile([P, BANK_HEADS, HEAD], F32, tag="heads")
            rotate_heads(nc, stage, q_banks[n], table, heads)
            store_heads(nc.sync, heads, out_0[:, n])

        v_bank = psum.tile([P, BANK], F32, tag="bank")
        for g in range(PASSES):
            if g < first_early:
                multiply(g, k_bank, kv_words[g], 0, Q_BANKS * BANK, False, g == first_early - 1)
            multiply(
                g, v_bank, kv_words[g], 1 if g < first_early else 0, (Q_BANKS + 1) * BANK,
                g == 0, g == PASSES - 1,
            )
        k_heads = results.tile([P, BANK_HEADS, HEAD], F32, tag="heads")
        rotate_heads(nc, stage, k_bank, table, k_heads)
        store_heads(nc.sync, k_heads, out_1)
        v_heads = results.tile([P, BANK_HEADS, HEAD], F32, tag="heads")
        nc.scalar.copy(out=v_heads[:].rearrange("p h d -> p (h d)"), in_=v_bank[:])
        store_heads(nc.scalar, v_heads, out_2)
